import numpy as np
import ml_dtypes


def mxq(x, axis, fmt="e4m3"):
    dtype, down = {"e4m3": (ml_dtypes.float8_e4m3fn, 7), "e5m2": (ml_dtypes.float8_e5m2, 14)}[fmt]
    v = np.moveaxis(np.asarray(x, np.float32).astype(ml_dtypes.bfloat16).astype(np.float64), axis, -1)
    blocks = v.reshape(v.shape[:-1] + (-1, 32))
    amax = np.abs(blocks).max(-1, keepdims=True)
    byte = np.maximum(np.where(amax > 0, np.frexp(amax)[1] - 1 + 127, 0) - down, 1)
    scale = np.exp2(byte - 127.0)
    codes = (blocks / scale).astype(np.float32).astype(dtype).astype(np.float64)
    return np.moveaxis((codes * scale).reshape(v.shape), -1, axis)


WIDE = False


def mx_kscale(k):
    if not WIDE:
        return np.ones(k)
    levels = np.array([10, -10, 5, -5, 0])
    if k % 512:
        return np.exp2(np.random.permutation(np.resize(levels, k // 32))).repeat(32)
    a = np.empty((k // 512, 16))
    for p in range(k // 512):
        a[p, :8] = np.random.permutation(np.resize(levels, 8))
        for g in range(8):
            far = levels[np.abs(levels - a[p, g]) >= 10]
            a[p, g + 8] = far[np.random.randint(len(far))]
    return np.exp2(a.ravel()).repeat(32)


BF16 = ml_dtypes.bfloat16


def bf(x):
    return np.asarray(x, np.float32).astype(BF16)


def f64(x):
    return np.asarray(x).astype(np.float64)


E2M1 = np.array([0.0, 0.5, 1.0, 1.5, 2.0, 3.0, 4.0, 6.0, -0.0, -0.5, -1.0, -1.5, -2.0, -3.0, -4.0, -6.0])


def pack_weight(w, fmt):
    k, n = w.shape
    w = f64(bf(w)).reshape(k // 32, 32, n)
    amax = np.abs(w).max(1)
    if fmt == "e4m3":
        byte = np.frexp(amax)[1] - 1 + 127 - 7
    else:
        mant, ex = np.frexp(amax / 6.0)
        byte = np.where(mant > 0.5, ex, ex - 1) + 127
    byte = np.clip(np.where(amax > 0, byte, 1), 1, 254)
    scaled = (w * np.exp2(127.0 - byte)[:, None, :]).reshape(k, n).astype(np.float32)
    by_word = np.ascontiguousarray(scaled.reshape(k // 512, 128, 4, n).transpose(0, 1, 3, 2))
    if fmt == "e4m3":
        words = by_word.astype(ml_dtypes.float8_e4m3fn).view(np.uint8)
    else:
        c = by_word.astype(ml_dtypes.float4_e2m1fn).view(np.uint8) & 0xF
        words = c[..., 0::2] | (c[..., 1::2] << 4)
    return np.ascontiguousarray(words), np.ascontiguousarray(byte.astype(np.uint8).reshape(k // 512, 16, n))


def unpack_weight(words, scales, fmt):
    g, p, n, _ = words.shape
    if fmt == "e4m3":
        vals = np.ascontiguousarray(words).view(ml_dtypes.float8_e4m3fn).astype(np.float64)
    else:
        nib = np.empty((g, p, n, 4), np.uint8)
        nib[..., 0::2] = words & 0xF
        nib[..., 1::2] = words >> 4
        vals = E2M1[nib]
    vals = vals * np.repeat(np.exp2(scales.astype(np.float64) - 127.0), 8, axis=1)[..., None]
    return vals.transpose(0, 1, 3, 2).reshape(g * 512, n)


H, D, L = 4, 512, 1024
HD = H * D


def split_heads(x):
    return x.reshape(L, H, D).transpose(1, 2, 0)


def draw0():
    s, t = mx_kscale(D), mx_kscale(L)
    tr = np.repeat(t, HD // L)
    e = np.exp(1.5 * np.random.standard_normal((H, L, L)))
    tokens = bf(np.random.standard_normal((D, L)) * s[:, None])
    Wv = np.random.standard_normal((HD, D)) * 0.5 / np.sqrt(D) / s * tr[:, None]
    words, scales = pack_weight(Wv.T, "e4m3")
    return {"attn": bf(e / e.sum(0, keepdims=True) / t),
            "tokens": tokens,
            "Wv_words": words,
            "Wv_scales": scales,
            "bv": bf(np.random.standard_normal(HD) * 0.15 * tr)}


def core(attn, tokens, Wv_words, Wv_scales, bv):
    v = split_heads((unpack_weight(Wv_words, Wv_scales, "e4m3").T @ mxq(f64(tokens), 0, "e4m3")) + f64(bv)[:, None])
    return mxq(v, 2, "e4m3") @ mxq(f64(attn).transpose(0, 2, 1), 1, "e4m3")


def e4m3fn_bytes(y):
    return np.clip(np.asarray(y, np.float64), -448.0, 448.0).astype(np.float32).astype(ml_dtypes.float8_e4m3fn).view(np.uint8)


def e4m3fn_values(b):
    return np.asarray(b, np.uint8).view(ml_dtypes.float8_e4m3fn).astype(np.float64)


def setup_inputs():
    d = draw0()
    x0 = np.asarray(d['attn']).astype(np.float64)
    s = (np.max(np.abs(x0), axis=(0, 1), keepdims=True) / 448.0).astype(np.float32)
    out = {}
    for k, v in d.items():
        if k == 'attn':
            out['attn_bytes'] = e4m3fn_bytes(x0 / s.astype(np.float64))
            out['attn_scale'] = s
        else:
            out[k] = v
    return out


def reference(attn_bytes, attn_scale, tokens, Wv_words, Wv_scales, bv):
    return core(e4m3fn_values(attn_bytes) * attn_scale.astype(np.float64), tokens, Wv_words, Wv_scales, bv)

@@ -1,0 +1,306 @@
+from contextlib import ExitStack
+
+import concourse.mybir as mybir
+from concourse.masks import make_identity
+
+H, D, L, C = 4, 512, 1024, 512
+FLOPS = 2 * (H * D) * C * L + 2 * H * D * L * L
+
+F32 = mybir.dt.float32
+BF16 = mybir.dt.bfloat16
+I32 = mybir.dt.int32
+U32 = mybir.dt.uint32
+U8 = mybir.dt.uint8
+FP8 = mybir.dt.float8_e4m3fn
+FP8X4 = mybir.dt.float8_e4m3fn_x4
+MULT = mybir.AluOpType.mult
+IDENT = mybir.ActivationFunctionType.Identity
+P = 128
+
+
+def tile_selfattention_pb_t_w8_kernel(tc, attn_bytes, attn_scale, tokens, Wv_words, Wv_scales, bv, out):
+    nc = tc.nc
+    with ExitStack() as ctx:
+        keep = ctx.enter_context(tc.tile_pool(name="keep", bufs=1))
+        work = ctx.enter_context(tc.tile_pool(name="work", bufs=2))
+        psum = ctx.enter_context(tc.psum_pool(name="psum", bufs=2))
+        ctx.enter_context(tc.manual_schedule())
+
+        srow = keep.tile([P, L], F32, name="srow")
+        ones = keep.tile([P, P], F32, name="ones")
+        identf = keep.tile([P, P], F32, name="identf")
+        sb = keep.tile([P, L], F32, name="sb", align_bytes=64)
+        w_raw = keep.tile([P, 2048], I32, name="w_raw", align_bytes=64)
+        ws_raw = keep.tile([P, 1024], U8, name="ws_raw", align_bytes=64)
+        w_perm = keep.tile([P, 2, 2, 4, P], I32, name="w_perm", align_bytes=64)
+        ws_perm = keep.tile([P, 2, 4, P], U8, name="ws_perm", align_bytes=64)
+        bias_raw = keep.tile([P, 2, 8], BF16, name="bias_raw")
+        bias = keep.tile([P, 16], F32, name="bias")
+        dummy = keep.tile([P, 8], F32, name="dummy")
+
+        nc.vector.memset(srow[:], 0.0)
+        nc.vector.memset(ws_raw[:].bitcast(I32), 0)
+        nc.gpsimd.memset(ones[:], 1.0)
+        make_identity(nc, identf[:])
+        nc.vector.memset(dummy[:], 0.0)
+
+        nc.scalar.dma_start(out=srow[0:1, :], in_=attn_scale[0])
+        nc.scalar.activation(out=dummy[:], in_=dummy[:], func=IDENT)
+        nc.scalar.dma_start(out=bias_raw[:], in_=bv.rearrange("(g q s) -> q g s", g=2, s=8))
+        nc.gpsimd.tensor_copy(out=bias[:], in_=bias_raw[:].rearrange("p g s -> p (g s)"))
+
+        tok_view = tokens.rearrange("(p t) c -> p t c", t=4)
+        tok_raw = [keep.tile([P, 4, 512], BF16, name="tok_raw%d" % i, align_bytes=64) for i in range(2)]
+        raw = [keep.tile([P, 4, L], U8, name="attn_raw%d" % i, align_bytes=64) for i in range(8)]
+
+        def load_attn(grp, j0, j1):
+            h, lh = grp // 2, grp % 2
+            nc.sync.dma_start(
+                out=raw[grp][:, j0:j1, :],
+                in_=attn_bytes[h, 512 * lh + 128 * j0 : 512 * lh + 128 * j1, :].rearrange("(j p) m -> p j m", p=P),
+            )
+
+        w_view = Wv_words[0].rearrange("p n t -> p (n t)").bitcast(I32)
+        nc.sync.dma_start(out=tok_raw[0][:], in_=tok_view[:, :, 0:512])
+        for q in range(4):
+            for g in range(2):
+                nc.sync.dma_start(
+                    out=ws_raw[32 * q + 4 * g : 32 * q + 4 * g + 4, :].bitcast(I32),
+                    in_=Wv_scales[0, 4 * q : 4 * q + 4, 1024 * g : 1024 * g + 1024].bitcast(I32),
+                )
+        nc.sync.dma_start(out=w_raw[:, 0:1024], in_=w_view[:, 0:1024])
+        nc.sync.dma_start(out=w_raw[:, 1024:2048], in_=w_view[:, 1024:2048])
+        load_attn(0, 0, 2)
+        nc.sync.dma_start(out=tok_raw[1][:], in_=tok_view[:, :, 512:1024])
+        load_attn(0, 2, 4)
+        for grp in range(1, 8):
+            load_attn(grp, 0, 4)
+
+        tok_code, tok_plane, tok_grp = {}, {}, {}
+        wid, trp, grpd, a_code, a_plane = {}, {}, {}, {}, {}
+        v_flat, v_grp, v_code, v_plane = {}, {}, {}, {}
+        outs = {}
+
+        blocks = [(b // 2, 512 * (b % 2), 512) for b in range(7)] + [(3, 512, 256), (3, 768, 128), (3, 896, 128)]
+
+        def block_of(u):
+            return u // 4 if u < 28 else (7, 7, 8, 9)[u - 28]
+
+        def bcast():
+            for i in range(2):
+                bc = psum.tile([P, 512], F32, name="pv", bufs=2)
+                nc.tensor.matmul(out=bc[:], lhsT=ones[:], rhs=srow[:, 512 * i : 512 * i + 512], start=True, stop=True)
+                nc.scalar.copy(out=sb[:, 512 * i : 512 * i + 512], in_=bc[:])
+
+        def tok_interleave(half, cut):
+            t = keep.tile([P, 512, 4], BF16, name="tok_grp%d" % half, align_bytes=64)
+            tok_grp[half] = t
+            src = tok_raw[half][:].rearrange("p t c -> p c t")
+            if cut > 0:
+                nc.vector.tensor_copy(out=t[:, :cut, :], in_=src[:, :cut, :])
+            nc.scalar.copy(out=t[:, cut:, :], in_=src[:, cut:, :])
+
+        def tok_quant(half):
+            c = keep.tile([P, 512], U32, name="tok_code%d" % half, align_bytes=64)
+            s = keep.tile([P, 512], U8, name="tok_plane%d" % half, align_bytes=64)
+            tok_code[half], tok_plane[half] = c, s
+            nc.vector.quantize_mx(out=c[:].bitcast(FP8X4), scales=s[:], in_=tok_grp[half][:].rearrange("p c t -> p (c t)"))
+
+        def w_permute(hh, gs):
+            for g in gs:
+                nc.vector.tensor_copy(
+                    out=w_perm[:, hh, g],
+                    in_=w_raw[:, 1024 * g : 1024 * g + 1024].rearrange("p (q t e) -> p e t q", t=4, e=2)[:, hh],
+                )
+            if 1 in gs:
+                nc.vector.tensor_copy(
+                    out=ws_perm[:, hh], in_=ws_raw[:].rearrange("p (q t e) -> p e t q", t=4, e=2)[:, hh]
+                )
+
+        def widen(u):
+            grp, j = u // 4, u % 4
+            w = work.tile([P, L], BF16, name="wid", bufs=6, align_bytes=64)
+            wid[u] = w
+            nc.vector.tensor_tensor(out=w[:], in0=raw[grp][:, j, :].bitcast(FP8), in1=sb[:], op=MULT)
+
+        def transposes(u, gs=(0, 1)):
+            t = psum.tile([P, len(gs), 2, P], F32, name="tr", bufs=3)
+            words = wid[u][:].bitcast(F32)
+            for n, g in enumerate(gs):
+                for e in range(2):
+                    nc.tensor.transpose(t[:, n, e, :], words[:, 256 * g + e : 256 * (g + 1) : 2], identf[:])
+            trp[u, gs] = t
+
+        def empty(u, eng="s", gs=(0, 1)):
+            b = block_of(u)
+            width = blocks[b][2]
+            if b not in grpd:
+                grpd[b] = work.tile([P, 2, width, 2], F32, name="grpd", bufs=3, align_bytes=64)
+            c = 128 * (u % 4) % width
+            o = grpd[b][:, gs[0] : gs[-1] + 1, c : c + 128, :]
+            i = trp[u, gs][:].rearrange("p g e l -> p g l e")
+            if eng == "s":
+                nc.scalar.copy(out=o, in_=i)
+            else:
+                nc.vector.tensor_copy(out=o, in_=i)
+
+        def attn_quant(b):
+            width = blocks[b][2]
+            a_code[b] = work.tile([P, 2, width], U32, name="a_code", bufs=3, align_bytes=64)
+            a_plane[b] = work.tile([P, 2, width], U8, name="a_plane", bufs=3, align_bytes=64)
+            nc.vector.quantize_mx(
+                out=a_code[b][:].rearrange("p g l -> p (g l)").bitcast(FP8X4),
+                scales=a_plane[b][:].rearrange("p g l -> p (g l)"),
+                in_=grpd[b][:].rearrange("p g l e -> p (g l e)").bitcast(BF16),
+            )
+
+        def project(h, i):
+            g, t, hh, half = i // 4, i % 4, h // 2, h % 2
+            if i == 0:
+                v_flat[h] = work.tile([P, 2, 4, 512], BF16, name="v_flat", bufs=2, align_bytes=64)
+            pv = psum.tile([P, 512], F32, name="pv", bufs=2)
+            nc.tensor.matmul_mx(
+                out=pv[:],
+                lhsT=w_perm[:, hh, g, t, :].bitcast(FP8X4),
+                lhsT_scale=ws_perm[4 * g : P, hh, t, :],
+                rhs=tok_code[half][:].bitcast(FP8X4),
+                rhs_scale=tok_plane[half][:],
+                start=True,
+                stop=True,
+            )
+            b = 8 * g + 2 * t + hh
+            nc.scalar.activation(out=v_flat[h][:, g, t, :], in_=pv[:], func=IDENT, bias=bias[:, b : b + 1])
+
+        def v_interleave(h, g, c0, c1, eng):
+            if (h, g) not in v_grp:
+                v_grp[h, g] = work.tile([P, 512, 4], BF16, name="v_grp", bufs=3, align_bytes=64)
+            if c0 == c1:
+                return
+            o = v_grp[h, g][:, c0:c1, :].rearrange("p (c i) t -> p c t i", i=4)
+            i = v_flat[h][:, g, :, c0:c1].rearrange("p t (c i) -> p c t i", i=4)
+            if eng == "s":
+                nc.scalar.copy(out=o, in_=i)
+            else:
+                nc.vector.tensor_copy(out=o, in_=i)
+
+        def v_quant(h, g):
+            if g == 0:
+                v_code[h] = work.tile([P, 2, 512], U32, name="v_code", bufs=2, align_bytes=64)
+                v_plane[h] = work.tile([P, 2, 512], U8, name="v_plane", bufs=2, align_bytes=64)
+            nc.vector.quantize_mx(
+                out=v_code[h][:, g].bitcast(FP8X4),
+                scales=v_plane[h][:, g],
+                in_=v_grp[h, g][:].rearrange("p c t -> p (c t)"),
+            )
+
+        def mix(b, d0, nd, eng="s"):
+            h, row, width = blocks[b]
+            acc = psum.tile([P, nd, width], F32, name="acc", bufs=3)
+            for a in range(nd):
+                dt = d0 + a
+                for g in range(2):
+                    nc.tensor.matmul_mx(
+                        out=acc[:, a, :],
+                        lhsT=v_code[h][:, g, 128 * dt : 128 * dt + 128].bitcast(FP8X4),
+                        lhsT_scale=v_plane[h][:, g, 128 * dt : 128 * dt + 128],
+                        rhs=a_code[b][:, g, :].bitcast(FP8X4),
+                        rhs_scale=a_plane[b][:, g, :],
+                        start=(g == 0),
+                        stop=(g == 1),
+                    )
+            pair = 2 if nd == 1 else nd
+            at = d0 % pair
+            if at == 0:
+                outs[b] = work.tile([P, pair, width], F32, name="outs", bufs=8)
+            if eng == "s":
+                nc.scalar.copy(out=outs[b][:, at : at + nd, :], in_=acc[:])
+            else:
+                nc.vector.tensor_copy(out=outs[b][:, at : at + nd, :], in_=acc[:])
+            if at + nd == pair:
+                e = d0 + nd
+                nc.sync.dma_start(
+                    out=out[h, 128 * (e - pair) : 128 * e, row : row + width].rearrange("(a p) l -> p a l", p=P),
+                    in_=outs[b][:],
+                )
+
+        V_SPLIT = 384
+        tok_interleave(0, 320)
+        bcast()
+        w_permute(0, (0,))
+        tok_quant(0)
+        w_permute(0, (1,))
+        for i in range(8):
+            project(0, i)
+        widen(0)
+        widen(1)
+
+        for k in range(14):
+            transposes(2 * k)
+            transposes(2 * k + 1)
+            empty(2 * k)
+            empty(2 * k + 1)
+            todo = []
+            if k == 1:
+                todo = [(0, 0), (0, 1)]
+            elif k % 2 == 1 and k < 14:
+                todo = [((k + 1) // 4, 0)] if k % 4 == 3 else [((k - 1) // 4, 1)]
+            todo = [x for x in todo if x[0] < 4]
+            for h, g in todo:
+                v_interleave(h, g, V_SPLIT, 512, "s")
+            if k == 0:
+                tok_interleave(1, 0)
+                widen(2)
+                widen(3)
+                w_permute(1, (0, 1))
+            elif k % 2 == 1:
+                widen(2 * k + 2)
+                for h, g in todo:
+                    v_interleave(h, g, 0, V_SPLIT, "v")
+                widen(2 * k + 3)
+                if k == 1:
+                    tok_quant(1)
+                pending = todo
+            else:
+                for h, g in pending:
+                    v_quant(h, g)
+                widen(2 * k + 2)
+                attn_quant(k // 2 - 1)
+                widen(2 * k + 3)
+            if k >= 3:
+                b, d0 = (k - 3) // 2, 0 if k % 2 == 1 else 2
+                mix(b, d0, 1)
+                mix(b, d0 + 1, 1)
+            if 1 <= k <= 12:
+                h, i = (k + 3) // 4, 2 * ((k - 1) % 4)
+                for i in range(0, 4) if k == 2 else () if k == 1 else (i, i + 1):
+                    project(h, i)
+
+        for h, g in pending:
+            v_quant(h, g)
+        transposes(28)
+        transposes(29)
+        empty(28)
+        empty(29)
+        attn_quant(6)
+        widen(30)
+        attn_quant(7)
+        widen(31)
+        mix(5, 2, 1)
+        mix(5, 3, 1)
+        mix(6, 0, 1)
+        mix(6, 1, 1)
+        transposes(30)
+        empty(30)
+        mix(6, 2, 1, "s")
+        mix(6, 3, 1, "s")
+        mix(7, 0, 2)
+        attn_quant(8)
+        transposes(31, (0,))
+        transposes(31, (1,))
+        empty(31, "v", (0,))
+        empty(31, "s", (1,))
+        attn_quant(9)
+        mix(7, 2, 2, "v")
+        mix(8, 0, 4, "s")
+        mix(9, 0, 2, "v")
+        mix(9, 2, 2, "s")

@@ -38,8 +38,8 @@ def tile_selfattention_pb_t_w8_kernel(tc, attn_bytes, attn_scale, tokens, Wv_wor
         bias = keep.tile([P, 16], F32, name="bias")
         dummy = keep.tile([P, 8], F32, name="dummy")
 
-        nc.vector.memset(srow[:], 0.0)
         nc.vector.memset(ws_raw[:].bitcast(I32), 0)
+        nc.vector.memset(srow[:], 0.0)
         nc.gpsimd.memset(ones[:], 1.0)
         make_identity(nc, identf[:])
         nc.vector.memset(dummy[:], 0.0)
@@ -61,13 +61,12 @@ def tile_selfattention_pb_t_w8_kernel(tc, attn_bytes, attn_scale, tokens, Wv_wor
             )
 
         w_view = Wv_words[0].rearrange("p n t -> p (n t)").bitcast(I32)
-        nc.sync.dma_start(out=tok_raw[0][:], in_=tok_view[:, :, 0:512])
         for q in range(4):
-            for g in range(2):
-                nc.sync.dma_start(
-                    out=ws_raw[32 * q + 4 * g : 32 * q + 4 * g + 4, :].bitcast(I32),
-                    in_=Wv_scales[0, 4 * q : 4 * q + 4, 1024 * g : 1024 * g + 1024].bitcast(I32),
-                )
+            nc.sync.dma_start(
+                out=ws_raw[32 * q : 32 * q + 8, :].bitcast(I32),
+                in_=Wv_scales[0, 4 * q : 4 * q + 4, :].bitcast(I32).rearrange("i (g n) -> g i n", g=2),
+            )
+        nc.sync.dma_start(out=tok_raw[0][:], in_=tok_view[:, :, 0:512])
         nc.sync.dma_start(out=w_raw[:, 0:1024], in_=w_view[:, 0:1024])
         nc.sync.dma_start(out=w_raw[:, 1024:2048], in_=w_view[:, 1024:2048])
         load_attn(0, 0, 2)
@@ -106,16 +105,16 @@ def tile_selfattention_pb_t_w8_kernel(tc, attn_bytes, attn_scale, tokens, Wv_wor
             tok_code[half], tok_plane[half] = c, s
             nc.vector.quantize_mx(out=c[:].bitcast(FP8X4), scales=s[:], in_=tok_grp[half][:].rearrange("p c t -> p (c t)"))
 
-        def w_permute(hh, gs):
-            for g in gs:
-                nc.vector.tensor_copy(
-                    out=w_perm[:, hh, g],
-                    in_=w_raw[:, 1024 * g : 1024 * g + 1024].rearrange("p (q t e) -> p e t q", t=4, e=2)[:, hh],
-                )
-            if 1 in gs:
-                nc.vector.tensor_copy(
-                    out=ws_perm[:, hh], in_=ws_raw[:].rearrange("p (q t e) -> p e t q", t=4, e=2)[:, hh]
-                )
+        def w_permute(g, a):
+            nc.vector.tensor_copy(
+                out=w_perm[:, :, g, 2 * a : 2 * a + 2, :].rearrange("p e t q -> p q t e"),
+                in_=w_raw[:, 1024 * g : 1024 * g + 1024].rearrange("p (q a t e) -> p a q t e", a=2, t=2, e=2)[:, a],
+            )
+
+        def ws_permute(hh):
+            nc.vector.tensor_copy(
+                out=ws_perm[:, hh], in_=ws_raw[:].rearrange("p (q t e) -> p e t q", t=4, e=2)[:, hh]
+            )
 
         def widen(u):
             grp, j = u // 4, u % 4
@@ -226,9 +225,11 @@ def tile_selfattention_pb_t_w8_kernel(tc, attn_bytes, attn_scale, tokens, Wv_wor
         V_SPLIT = 384
         tok_interleave(0, 320)
         bcast()
-        w_permute(0, (0,))
+        ws_permute(0)
         tok_quant(0)
-        w_permute(0, (1,))
+        for g in range(2):
+            for a in range(2):
+                w_permute(g, a)
         for i in range(8):
             project(0, i)
         widen(0)
@@ -251,7 +252,7 @@ def tile_selfattention_pb_t_w8_kernel(tc, attn_bytes, attn_scale, tokens, Wv_wor
                 tok_interleave(1, 0)
                 widen(2)
                 widen(3)
-                w_permute(1, (0, 1))
+                ws_permute(1)
             elif k % 2 == 1:
                 widen(2 * k + 2)
                 for h, g in todo:

@@ -61,12 +61,13 @@ def tile_selfattention_pb_t_w8_kernel(tc, attn_bytes, attn_scale, tokens, Wv_wor
             )
 
         w_view = Wv_words[0].rearrange("p n t -> p (n t)").bitcast(I32)
+        for c in range(2):
+            nc.sync.dma_start(out=tok_raw[0][:, :, 256 * c : 256 * c + 256], in_=tok_view[:, :, 256 * c : 256 * c + 256])
         for q in range(4):
             nc.sync.dma_start(
                 out=ws_raw[32 * q : 32 * q + 8, :].bitcast(I32),
                 in_=Wv_scales[0, 4 * q : 4 * q + 4, :].bitcast(I32).rearrange("i (g n) -> g i n", g=2),
             )
-        nc.sync.dma_start(out=tok_raw[0][:], in_=tok_view[:, :, 0:512])
         nc.sync.dma_start(out=w_raw[:, 0:1024], in_=w_view[:, 0:1024])
         nc.sync.dma_start(out=w_raw[:, 1024:2048], in_=w_view[:, 1024:2048])
         load_attn(0, 0, 2)
@@ -91,9 +92,13 @@ def tile_selfattention_pb_t_w8_kernel(tc, attn_bytes, attn_scale, tokens, Wv_wor
                 nc.tensor.matmul(out=bc[:], lhsT=ones[:], rhs=srow[:, 512 * i : 512 * i + 512], start=True, stop=True)
                 nc.scalar.copy(out=sb[:, 512 * i : 512 * i + 512], in_=bc[:])
 
+        def filler(n):
+            for i in range(n):
+                f = psum.tile([P, 512], F32, name="pv", bufs=2)
+                nc.tensor.matmul(out=f[:, 0:P], lhsT=ones[:], rhs=ones[:], start=True, stop=True)
+
         def tok_interleave(half, cut):
-            t = keep.tile([P, 512, 4], BF16, name="tok_grp%d" % half, align_bytes=64)
-            tok_grp[half] = t
+            t = tok_grp[half] = keep.tile([P, 512, 4], BF16, name="tok_grp%d" % half, align_bytes=64)
             src = tok_raw[half][:].rearrange("p t c -> p c t")
             if cut > 0:
                 nc.vector.tensor_copy(out=t[:, :cut, :], in_=src[:, :cut, :])
@@ -223,7 +228,8 @@ def tile_selfattention_pb_t_w8_kernel(tc, attn_bytes, attn_scale, tokens, Wv_wor
                 )
 
         V_SPLIT = 384
-        tok_interleave(0, 320)
+        filler(5)
+        tok_interleave(0, 256)
         bcast()
         ws_permute(0)
         tok_quant(0)
@@ -237,8 +243,12 @@ def tile_selfattention_pb_t_w8_kernel(tc, attn_bytes, attn_scale, tokens, Wv_wor
 
         for k in range(14):
             transposes(2 * k)
-            transposes(2 * k + 1)
             empty(2 * k)
+            if k >= 3:
+                b, d0 = (k - 3) // 2, 0 if k % 2 == 1 else 2
+                mix(b, d0, 1)
+                mix(b, d0 + 1, 1)
+            transposes(2 * k + 1)
             empty(2 * k + 1)
             todo = []
             if k == 1:
@@ -267,10 +277,8 @@ def tile_selfattention_pb_t_w8_kernel(tc, attn_bytes, attn_scale, tokens, Wv_wor
                 widen(2 * k + 2)
                 attn_quant(k // 2 - 1)
                 widen(2 * k + 3)
-            if k >= 3:
-                b, d0 = (k - 3) // 2, 0 if k % 2 == 1 else 2
-                mix(b, d0, 1)
-                mix(b, d0 + 1, 1)
+            if k in (0, 1, 13):
+                filler(2)
             if 1 <= k <= 12:
                 h, i = (k + 3) // 4, 2 * ((k - 1) % 4)
                 for i in range(0, 4) if k == 2 else () if k == 1 else (i, i + 1):

@@ -227,89 +227,215 @@ def tile_selfattention_pb_t_w8_kernel(tc, attn_bytes, attn_scale, tokens, Wv_wor
                     in_=outs[b][:],
                 )
 
-        V_SPLIT = 384
-        filler(5)
         tok_interleave(0, 256)
-        bcast()
         ws_permute(0)
+        w_permute(0, 0)
         tok_quant(0)
-        for g in range(2):
-            for a in range(2):
-                w_permute(g, a)
-        for i in range(8):
-            project(0, i)
-        widen(0)
+        w_permute(1, 1)
+        filler(5)
+        bcast()
+        w_permute(1, 0)
+        project(0, 0)
+        project(0, 4)
+        w_permute(0, 1)
+        project(0, 7)
+        project(0, 1)
         widen(1)
-
-        for k in range(14):
-            transposes(2 * k)
-            empty(2 * k)
-            if k >= 3:
-                b, d0 = (k - 3) // 2, 0 if k % 2 == 1 else 2
-                mix(b, d0, 1)
-                mix(b, d0 + 1, 1)
-            transposes(2 * k + 1)
-            empty(2 * k + 1)
-            todo = []
-            if k == 1:
-                todo = [(0, 0), (0, 1)]
-            elif k % 2 == 1 and k < 14:
-                todo = [((k + 1) // 4, 0)] if k % 4 == 3 else [((k - 1) // 4, 1)]
-            todo = [x for x in todo if x[0] < 4]
-            for h, g in todo:
-                v_interleave(h, g, V_SPLIT, 512, "s")
-            if k == 0:
-                tok_interleave(1, 0)
-                widen(2)
-                widen(3)
-                ws_permute(1)
-            elif k % 2 == 1:
-                widen(2 * k + 2)
-                for h, g in todo:
-                    v_interleave(h, g, 0, V_SPLIT, "v")
-                widen(2 * k + 3)
-                if k == 1:
-                    tok_quant(1)
-                pending = todo
-            else:
-                for h, g in pending:
-                    v_quant(h, g)
-                widen(2 * k + 2)
-                attn_quant(k // 2 - 1)
-                widen(2 * k + 3)
-            if k in (0, 1, 13):
-                filler(2)
-            if 1 <= k <= 12:
-                h, i = (k + 3) // 4, 2 * ((k - 1) % 4)
-                for i in range(0, 4) if k == 2 else () if k == 1 else (i, i + 1):
-                    project(h, i)
-
-        for h, g in pending:
-            v_quant(h, g)
+        widen(0)
+        widen(3)
+        project(0, 5)
+        project(0, 6)
+        widen(4)
+        tok_interleave(1, 0)
+        transposes(0)
+        project(0, 2)
+        widen(2)
+        project(0, 3)
+        empty(0)
+        widen(5)
+        v_interleave(0, 1, 0, 320, 'v')
+        transposes(1)
+        widen(6)
+        transposes(2)
+        filler(2)
+        transposes(3)
+        empty(1)
+        transposes(4)
+        widen(8)
+        v_interleave(0, 0, 192, 512, 's')
+        empty(2, 's')
+        empty(3)
+        transposes(5)
+        ws_permute(1)
+        v_interleave(0, 0, 0, 192, 'v')
+        empty(4)
+        tok_quant(1)
+        widen(9)
+        v_interleave(0, 1, 320, 512, 's')
+        project(1, 0)
+        project(1, 3)
+        widen(7)
+        empty(5)
+        project(1, 2)
+        v_quant(0, 0)
+        project(1, 1)
+        attn_quant(0)
+        transposes(6)
+        v_quant(0, 1)
+        filler(2)
+        v_interleave(1, 0, 192, 512, 's')
+        mix(0, 0, 1)
+        mix(0, 1, 1)
+        empty(6)
+        v_interleave(1, 0, 0, 192, 'v')
+        project(1, 4)
+        transposes(7)
+        transposes(8)
+        widen(11)
+        project(1, 6)
+        mix(0, 2, 1)
+        project(1, 5)
+        transposes(9)
+        empty(8)
+        widen(10)
+        empty(7, 'v')
+        v_quant(1, 0)
+        project(1, 7)
+        attn_quant(1)
+        transposes(10)
+        widen(13)
+        v_interleave(1, 1, 352, 512, 's')
+        mix(0, 3, 1)
+        transposes(11)
+        empty(9)
+        widen(12)
+        project(2, 0)
+        empty(11)
+        widen(15)
+        widen(18)
+        mix(1, 0, 1)
+        mix(1, 1, 1)
+        transposes(12)
+        v_interleave(1, 1, 0, 352, 'v')
+        empty(10)
+        mix(1, 2, 1)
+        mix(1, 3, 1)
+        project(2, 2)
+        transposes(13)
+        empty(12, 's')
+        project(2, 3)
+        widen(16)
+        attn_quant(2)
+        v_quant(1, 1)
+        project(2, 1)
+        mix(2, 0, 1)
+        widen(14)
+        widen(19)
+        v_interleave(2, 0, 448, 512, 's')
+        mix(2, 1, 1)
+        project(2, 5)
+        widen(17)
+        transposes(15)
+        transposes(14)
+        empty(15)
+        empty(14, 'v')
+        empty(13)
+        project(2, 4)
+        mix(2, 2, 1)
+        v_interleave(2, 0, 0, 448, 'v')
+        attn_quant(3)
+        project(2, 6)
+        mix(2, 3, 1)
+        transposes(17)
+        transposes(16)
+        empty(16)
+        project(2, 7)
+        transposes(18)
+        empty(17)
+        project(3, 0)
+        widen(20)
+        mix(3, 0, 1)
+        v_quant(2, 0)
+        mix(3, 1, 1)
+        transposes(19)
+        widen(21)
+        v_interleave(2, 1, 0, 416, 'v')
+        widen(22)
+        v_interleave(2, 1, 416, 512, 's')
+        empty(18)
+        empty(19)
+        v_quant(2, 1)
+        project(3, 3)
+        attn_quant(4)
+        project(3, 1)
+        transposes(20)
+        empty(20)
+        mix(3, 2, 1)
+        mix(3, 3, 1)
+        transposes(21)
+        project(3, 2)
+        mix(4, 0, 1)
+        widen(23)
+        mix(4, 1, 1)
+        transposes(23)
+        empty(23)
+        transposes(22)
+        empty(21)
+        widen(24)
+        project(3, 4)
+        widen(26)
+        empty(22)
+        mix(4, 2, 1)
+        v_interleave(3, 0, 0, 416, 'v')
+        widen(25)
+        transposes(24)
+        empty(24)
+        project(3, 5)
+        project(3, 6)
+        mix(4, 3, 1)
+        transposes(25)
+        attn_quant(5)
+        transposes(26)
+        empty(25)
+        project(3, 7)
+        empty(26)
+        widen(27)
+        mix(5, 0, 1)
+        transposes(27)
+        widen(28)
+        v_interleave(3, 0, 416, 512, 's')
+        empty(27)
+        widen(29)
+        v_interleave(3, 1, 0, 416, 'v')
+        v_interleave(3, 1, 416, 512, 's')
+        v_quant(3, 0)
         transposes(28)
-        transposes(29)
-        empty(28)
-        empty(29)
         attn_quant(6)
-        widen(30)
-        attn_quant(7)
-        widen(31)
+        v_quant(3, 1)
+        mix(5, 1, 1)
+        empty(28)
         mix(5, 2, 1)
+        transposes(29)
         mix(5, 3, 1)
+        empty(29)
+        widen(30)
+        filler(2)
         mix(6, 0, 1)
+        attn_quant(7)
         mix(6, 1, 1)
+        widen(31)
         transposes(30)
-        empty(30)
-        mix(6, 2, 1, "s")
-        mix(6, 3, 1, "s")
-        mix(7, 0, 2)
+        mix(6, 2, 1, 'v')
+        empty(30, 'v')
+        mix(6, 3, 1, 's')
         attn_quant(8)
         transposes(31, (0,))
         transposes(31, (1,))
-        empty(31, "v", (0,))
-        empty(31, "s", (1,))
+        mix(7, 2, 2, 's')
+        empty(31, 'v', (1,))
+        mix(7, 0, 2)
+        empty(31, 'v', (0,))
         attn_quant(9)
-        mix(7, 2, 2, "v")
-        mix(8, 0, 4, "s")
-        mix(9, 0, 2, "v")
-        mix(9, 2, 2, "s")
+        mix(8, 0, 4, 's')
+        mix(9, 0, 2, 'v')
+        mix(9, 2, 2, 'v')

from contextlib import ExitStack

import concourse.mybir as mybir
from concourse.masks import make_identity

H, D, L, C = 4, 512, 1024, 512
FLOPS = 2 * (H * D) * C * L + 2 * H * D * L * L

F32 = mybir.dt.float32
BF16 = mybir.dt.bfloat16
I32 = mybir.dt.int32
U32 = mybir.dt.uint32
U8 = mybir.dt.uint8
FP8 = mybir.dt.float8_e4m3fn
FP8X4 = mybir.dt.float8_e4m3fn_x4
MULT = mybir.AluOpType.mult
IDENT = mybir.ActivationFunctionType.Identity
P = 128


def tile_selfattention_pb_t_w8_kernel(tc, attn_bytes, attn_scale, tokens, Wv_words, Wv_scales, bv, out):
    nc = tc.nc
    with ExitStack() as ctx:
        keep = ctx.enter_context(tc.tile_pool(name="keep", bufs=1))
        work = ctx.enter_context(tc.tile_pool(name="work", bufs=2))
        psum = ctx.enter_context(tc.psum_pool(name="psum", bufs=2))
        ctx.enter_context(tc.manual_schedule())

        srow = keep.tile([P, L], F32, name="srow")
        ones = keep.tile([P, P], F32, name="ones")
        identf = keep.tile([P, P], F32, name="identf")
        sb = keep.tile([P, L], F32, name="sb", align_bytes=64)
        w_raw = keep.tile([P, 2048], I32, name="w_raw", align_bytes=64)
        ws_raw = keep.tile([P, 1024], U8, name="ws_raw", align_bytes=64)
        w_perm = keep.tile([P, 2, 2, 4, P], I32, name="w_perm", align_bytes=64)
        ws_perm = keep.tile([P, 2, 4, P], U8, name="ws_perm", align_bytes=64)
        bias_raw = keep.tile([P, 2, 8], BF16, name="bias_raw")
        bias = keep.tile([P, 16], F32, name="bias")
        dummy = keep.tile([P, 8], F32, name="dummy")

        nc.vector.memset(ws_raw[:].bitcast(I32), 0)
        nc.vector.memset(srow[:], 0.0)
        nc.gpsimd.memset(ones[:], 1.0)
        make_identity(nc, identf[:])
        nc.vector.memset(dummy[:], 0.0)

        nc.scalar.dma_start(out=srow[0:1, :], in_=attn_scale[0])
        nc.scalar.activation(out=dummy[:], in_=dummy[:], func=IDENT)
        nc.scalar.dma_start(out=bias_raw[:], in_=bv.rearrange("(g q s) -> q g s", g=2, s=8))
        nc.gpsimd.tensor_copy(out=bias[:], in_=bias_raw[:].rearrange("p g s -> p (g s)"))

        tok_view = tokens.rearrange("(p t) c -> p t c", t=4)
        tok_raw = [keep.tile([P, 4, 512], BF16, name="tok_raw%d" % i, align_bytes=64) for i in range(2)]
        raw = [keep.tile([P, 4, L], U8, name="attn_raw%d" % i, align_bytes=64) for i in range(8)]

        def load_attn(grp, j0, j1):
            h, lh = grp // 2, grp % 2
            nc.sync.dma_start(
                out=raw[grp][:, j0:j1, :],
                in_=attn_bytes[h, 512 * lh + 128 * j0 : 512 * lh + 128 * j1, :].rearrange("(j p) m -> p j m", p=P),
            )

        w_view = Wv_words[0].rearrange("p n t -> p (n t)").bitcast(I32)
        for c in range(2):
            nc.sync.dma_start(out=tok_raw[0][:, :, 256 * c : 256 * c + 256], in_=tok_view[:, :, 256 * c : 256 * c + 256])
        for q in range(4):
            nc.sync.dma_start(
                out=ws_raw[32 * q : 32 * q + 8, :].bitcast(I32),
                in_=Wv_scales[0, 4 * q : 4 * q + 4, :].bitcast(I32).rearrange("i (g n) -> g i n", g=2),
            )
        nc.sync.dma_start(out=w_raw[:, 0:1024], in_=w_view[:, 0:1024])
        nc.sync.dma_start(out=w_raw[:, 1024:2048], in_=w_view[:, 1024:2048])
        load_attn(0, 0, 2)
        nc.sync.dma_start(out=tok_raw[1][:], in_=tok_view[:, :, 512:1024])
        load_attn(0, 2, 4)
        for grp in range(1, 8):
            load_attn(grp, 0, 4)

        tok_code, tok_plane, tok_grp = {}, {}, {}
        wid, trp, grpd, a_code, a_plane = {}, {}, {}, {}, {}
        v_flat, v_grp, v_code, v_plane = {}, {}, {}, {}
        outs = {}

        blocks = [(b // 2, 512 * (b % 2), 512) for b in range(7)] + [(3, 512, 256), (3, 768, 128), (3, 896, 128)]

        def block_of(u):
            return u // 4 if u < 28 else (7, 7, 8, 9)[u - 28]

        def bcast():
            for i in range(2):
                bc = psum.tile([P, 512], F32, name="pv", bufs=2)
                nc.tensor.matmul(out=bc[:], lhsT=ones[:], rhs=srow[:, 512 * i : 512 * i + 512], start=True, stop=True)
                nc.scalar.copy(out=sb[:, 512 * i : 512 * i + 512], in_=bc[:])

        def filler(n):
            for i in range(n):
                f = psum.tile([P, 512], F32, name="pv", bufs=2)
                nc.tensor.matmul(out=f[:, 0:P], lhsT=ones[:], rhs=ones[:], start=True, stop=True)

        def tok_interleave(half, cut):
            t = tok_grp[half] = keep.tile([P, 512, 4], BF16, name="tok_grp%d" % half, align_bytes=64)
            src = tok_raw[half][:].rearrange("p t c -> p c t")
            if cut > 0:
                nc.vector.tensor_copy(out=t[:, :cut, :], in_=src[:, :cut, :])
            nc.scalar.copy(out=t[:, cut:, :], in_=src[:, cut:, :])

        def tok_quant(half):
            c = keep.tile([P, 512], U32, name="tok_code%d" % half, align_bytes=64)
            s = keep.tile([P, 512], U8, name="tok_plane%d" % half, align_bytes=64)
            tok_code[half], tok_plane[half] = c, s
            nc.vector.quantize_mx(out=c[:].bitcast(FP8X4), scales=s[:], in_=tok_grp[half][:].rearrange("p c t -> p (c t)"))

        def w_permute(g, a):
            nc.vector.tensor_copy(
                out=w_perm[:, :, g, 2 * a : 2 * a + 2, :].rearrange("p e t q -> p q t e"),
                in_=w_raw[:, 1024 * g : 1024 * g + 1024].rearrange("p (q a t e) -> p a q t e", a=2, t=2, e=2)[:, a],
            )

        def ws_permute(hh):
            nc.vector.tensor_copy(
                out=ws_perm[:, hh], in_=ws_raw[:].rearrange("p (q t e) -> p e t q", t=4, e=2)[:, hh]
            )

        def widen(u):
            grp, j = u // 4, u % 4
            w = work.tile([P, L], BF16, name="wid", bufs=6, align_bytes=64)
            wid[u] = w
            nc.vector.tensor_tensor(out=w[:], in0=raw[grp][:, j, :].bitcast(FP8), in1=sb[:], op=MULT)

        def transposes(u, gs=(0, 1)):
            t = psum.tile([P, len(gs), 2, P], F32, name="tr", bufs=3)
            words = wid[u][:].bitcast(F32)
            for n, g in enumerate(gs):
                for e in range(2):
                    nc.tensor.transpose(t[:, n, e, :], words[:, 256 * g + e : 256 * (g + 1) : 2], identf[:])
            trp[u, gs] = t

        def empty(u, eng="s", gs=(0, 1)):
            b = block_of(u)
            width = blocks[b][2]
            if b not in grpd:
                grpd[b] = work.tile([P, 2, width, 2], F32, name="grpd", bufs=3, align_bytes=64)
            c = 128 * (u % 4) % width
            o = grpd[b][:, gs[0] : gs[-1] + 1, c : c + 128, :]
            i = trp[u, gs][:].rearrange("p g e l -> p g l e")
            if eng == "s":
                nc.scalar.copy(out=o, in_=i)
            else:
                nc.vector.tensor_copy(out=o, in_=i)

        def attn_quant(b):
            width = blocks[b][2]
            a_code[b] = work.tile([P, 2, width], U32, name="a_code", bufs=3, align_bytes=64)
            a_plane[b] = work.tile([P, 2, width], U8, name="a_plane", bufs=3, align_bytes=64)
            nc.vector.quantize_mx(
                out=a_code[b][:].rearrange("p g l -> p (g l)").bitcast(FP8X4),
                scales=a_plane[b][:].rearrange("p g l -> p (g l)"),
                in_=grpd[b][:].rearrange("p g l e -> p (g l e)").bitcast(BF16),
            )

        def project(h, i):
            g, t, hh, half = i // 4, i % 4, h // 2, h % 2
            if i == 0:
                v_flat[h] = work.tile([P, 2, 4, 512], BF16, name="v_flat", bufs=2, align_bytes=64)
            pv = psum.tile([P, 512], F32, name="pv", bufs=2)
            nc.tensor.matmul_mx(
                out=pv[:],
                lhsT=w_perm[:, hh, g, t, :].bitcast(FP8X4),
                lhsT_scale=ws_perm[4 * g : P, hh, t, :],
                rhs=tok_code[half][:].bitcast(FP8X4),
                rhs_scale=tok_plane[half][:],
                start=True,
                stop=True,
            )
            b = 8 * g + 2 * t + hh
            nc.scalar.activation(out=v_flat[h][:, g, t, :], in_=pv[:], func=IDENT, bias=bias[:, b : b + 1])

        def v_interleave(h, g, c0, c1, eng):
            if (h, g) not in v_grp:
                v_grp[h, g] = work.tile([P, 512, 4], BF16, name="v_grp", bufs=3, align_bytes=64)
            if c0 == c1:
                return
            o = v_grp[h, g][:, c0:c1, :].rearrange("p (c i) t -> p c t i", i=4)
            i = v_flat[h][:, g, :, c0:c1].rearrange("p t (c i) -> p c t i", i=4)
            if eng == "s":
                nc.scalar.copy(out=o, in_=i)
            else:
                nc.vector.tensor_copy(out=o, in_=i)

        def v_quant(h, g):
            if g == 0:
                v_code[h] = work.tile([P, 2, 512], U32, name="v_code", bufs=2, align_bytes=64)
                v_plane[h] = work.tile([P, 2, 512], U8, name="v_plane", bufs=2, align_bytes=64)
            nc.vector.quantize_mx(
                out=v_code[h][:, g].bitcast(FP8X4),
                scales=v_plane[h][:, g],
                in_=v_grp[h, g][:].rearrange("p c t -> p (c t)"),
            )

        def mix(b, d0, nd, eng="s"):
            h, row, width = blocks[b]
            acc = psum.tile([P, nd, width], F32, name="acc", bufs=3)
            for a in range(nd):
                dt = d0 + a
                for g in range(2):
                    nc.tensor.matmul_mx(
                        out=acc[:, a, :],
                        lhsT=v_code[h][:, g, 128 * dt : 128 * dt + 128].bitcast(FP8X4),
                        lhsT_scale=v_plane[h][:, g, 128 * dt : 128 * dt + 128],
                        rhs=a_code[b][:, g, :].bitcast(FP8X4),
                        rhs_scale=a_plane[b][:, g, :],
                        start=(g == 0),
                        stop=(g == 1),
                    )
            pair = 2 if nd == 1 else nd
            at = d0 % pair
            if at == 0:
                outs[b] = work.tile([P, pair, width], F32, name="outs", bufs=8)
            if eng == "s":
                nc.scalar.copy(out=outs[b][:, at : at + nd, :], in_=acc[:])
            else:
                nc.vector.tensor_copy(out=outs[b][:, at : at + nd, :], in_=acc[:])
            if at + nd == pair:
                e = d0 + nd
                nc.sync.dma_start(
                    out=out[h, 128 * (e - pair) : 128 * e, row : row + width].rearrange("(a p) l -> p a l", p=P),
                    in_=outs[b][:],
                )

        tok_interleave(0, 256)
        ws_permute(0)
        w_permute(0, 0)
        tok_quant(0)
        w_permute(1, 1)
        filler(5)
        bcast()
        w_permute(1, 0)
        project(0, 0)
        project(0, 4)
        w_permute(0, 1)
        project(0, 7)
        project(0, 1)
        widen(1)
        widen(0)
        widen(3)
        project(0, 5)
        project(0, 6)
        widen(4)
        tok_interleave(1, 0)
        transposes(0)
        project(0, 2)
        widen(2)
        project(0, 3)
        empty(0)
        widen(5)
        v_interleave(0, 1, 0, 320, 'v')
        transposes(1)
        widen(6)
        transposes(2)
        filler(2)
        transposes(3)
        empty(1)
        transposes(4)
        widen(8)
        v_interleave(0, 0, 192, 512, 's')
        empty(2, 's')
        empty(3)
        transposes(5)
        ws_permute(1)
        v_interleave(0, 0, 0, 192, 'v')
        empty(4)
        tok_quant(1)
        widen(9)
        v_interleave(0, 1, 320, 512, 's')
        project(1, 0)
        project(1, 3)
        widen(7)
        empty(5)
        project(1, 2)
        v_quant(0, 0)
        project(1, 1)
        attn_quant(0)
        transposes(6)
        v_quant(0, 1)
        filler(2)
        v_interleave(1, 0, 192, 512, 's')
        mix(0, 0, 1)
        mix(0, 1, 1)
        empty(6)
        v_interleave(1, 0, 0, 192, 'v')
        project(1, 4)
        transposes(7)
        transposes(8)
        widen(11)
        project(1, 6)
        mix(0, 2, 1)
        project(1, 5)
        transposes(9)
        empty(8)
        widen(10)
        empty(7, 'v')
        v_quant(1, 0)
        project(1, 7)
        attn_quant(1)
        transposes(10)
        widen(13)
        v_interleave(1, 1, 352, 512, 's')
        mix(0, 3, 1)
        transposes(11)
        empty(9)
        widen(12)
        project(2, 0)
        empty(11)
        widen(15)
        widen(18)
        mix(1, 0, 1)
        mix(1, 1, 1)
        transposes(12)
        v_interleave(1, 1, 0, 352, 'v')
        empty(10)
        mix(1, 2, 1)
        mix(1, 3, 1)
        project(2, 2)
        transposes(13)
        empty(12, 's')
        project(2, 3)
        widen(16)
        attn_quant(2)
        v_quant(1, 1)
        project(2, 1)
        mix(2, 0, 1)
        widen(14)
        widen(19)
        v_interleave(2, 0, 448, 512, 's')
        mix(2, 1, 1)
        project(2, 5)
        widen(17)
        transposes(15)
        transposes(14)
        empty(15)
        empty(14, 'v')
        empty(13)
        project(2, 4)
        mix(2, 2, 1)
        v_interleave(2, 0, 0, 448, 'v')
        attn_quant(3)
        project(2, 6)
        mix(2, 3, 1)
        transposes(17)
        transposes(16)
        empty(16)
        project(2, 7)
        transposes(18)
        empty(17)
        project(3, 0)
        widen(20)
        mix(3, 0, 1)
        v_quant(2, 0)
        mix(3, 1, 1)
        transposes(19)
        widen(21)
        v_interleave(2, 1, 0, 416, 'v')
        widen(22)
        v_interleave(2, 1, 416, 512, 's')
        empty(18)
        empty(19)
        v_quant(2, 1)
        project(3, 3)
        attn_quant(4)
        project(3, 1)
        transposes(20)
        empty(20)
        mix(3, 2, 1)
        mix(3, 3, 1)
        transposes(21)
        project(3, 2)
        mix(4, 0, 1)
        widen(23)
        mix(4, 1, 1)
        transposes(23)
        empty(23)
        transposes(22)
        empty(21)
        widen(24)
        project(3, 4)
        widen(26)
        empty(22)
        mix(4, 2, 1)
        v_interleave(3, 0, 0, 416, 'v')
        widen(25)
        transposes(24)
        empty(24)
        project(3, 5)
        project(3, 6)
        mix(4, 3, 1)
        transposes(25)
        attn_quant(5)
        transposes(26)
        empty(25)
        project(3, 7)
        empty(26)
        widen(27)
        mix(5, 0, 1)
        transposes(27)
        widen(28)
        v_interleave(3, 0, 416, 512, 's')
        empty(27)
        widen(29)
        v_interleave(3, 1, 0, 416, 'v')
        v_interleave(3, 1, 416, 512, 's')
        v_quant(3, 0)
        transposes(28)
        attn_quant(6)
        v_quant(3, 1)
        mix(5, 1, 1)
        empty(28)
        mix(5, 2, 1)
        transposes(29)
        mix(5, 3, 1)
        empty(29)
        widen(30)
        filler(2)
        mix(6, 0, 1)
        attn_quant(7)
        mix(6, 1, 1)
        widen(31)
        transposes(30)
        mix(6, 2, 1, 'v')
        empty(30, 'v')
        mix(6, 3, 1, 's')
        attn_quant(8)
        transposes(31, (0,))
        transposes(31, (1,))
        mix(7, 2, 2, 's')
        empty(31, 'v', (1,))
        mix(7, 0, 2)
        empty(31, 'v', (0,))
        attn_quant(9)
        mix(8, 0, 4, 's')
        mix(9, 0, 2, 'v')
        mix(9, 2, 2, 'v')
